import numpy as np
import ml_dtypes


def mxq(x, axis, fmt="e4m3"):
    dtype, down = {"e4m3": (ml_dtypes.float8_e4m3fn, 7), "e5m2": (ml_dtypes.float8_e5m2, 14)}[fmt]
    v = np.moveaxis(np.asarray(x, np.float32).astype(ml_dtypes.bfloat16).astype(np.float64), axis, -1)
    blocks = v.reshape(v.shape[:-1] + (-1, 32))
    amax = np.abs(blocks).max(-1, keepdims=True)
    byte = np.maximum(np.where(amax > 0, np.frexp(amax)[1] - 1 + 127, 0) - down, 1)
    scale = np.exp2(byte - 127.0)
    codes = (blocks / scale).astype(np.float32).astype(dtype).astype(np.float64)
    return np.moveaxis((codes * scale).reshape(v.shape), -1, axis)


WIDE = False


def mx_kscale(k):
    if not WIDE:
        return np.ones(k)
    levels = np.array([10, -10, 5, -5, 0])
    a = np.random.permutation(np.resize(levels, k // 512 * 4)).reshape(k // 512, 4)
    idx = np.arange(k)
    return np.exp2(a[idx // 512, idx % 128 // 32])


BF16 = ml_dtypes.bfloat16


def bf(x):
    return np.asarray(x, np.float32).astype(BF16)


def f64(x):
    return np.asarray(x).astype(np.float64)


B, IN, H, OUT, L, STEPS = 1024, 512, 1024, 128, 3, 3
LN_EPS = 1e-5
TAU_EPS = 1e-6


def layer_norm(v, g, b):
    m = v.mean(-1, keepdims=True)
    var = ((v - m) ** 2).mean(-1, keepdims=True)
    return (v - m) / np.sqrt(var + LN_EPS) * g + b


def setup_inputs():
    r = mx_kscale(IN)
    s = mx_kscale(H)
    s = s / s.max()
    t = mx_kscale(H)
    liq_rms = np.sqrt(L * (L + 1) / 2.0)
    return {"liq": bf(np.random.standard_normal((B, H)) * liq_rms * s),
            "h": bf(np.random.standard_normal((B, H))),
            "x": bf(np.random.standard_normal((B, IN)) * r),
            "W_in": bf(np.random.standard_normal((H, IN)) * 0.7 / np.sqrt(IN) / r),
            "b_in": bf(np.random.standard_normal(H) * 0.3),
            "W_v": bf(np.random.standard_normal((H, H)) / np.sqrt(H) * t[:, None] / s),
            "b_v": bf(np.random.standard_normal(H) * 0.5 * t),
            "W_o": bf(np.random.standard_normal((H, H)) / np.sqrt(H) / t),
            "b_o": bf(np.random.standard_normal(H) * 0.5),
            "g_att": bf(1.0 + 0.1 * np.random.standard_normal(H)),
            "beta_att": bf(np.random.standard_normal(H) * 0.3),
            "tau": bf(0.5 + 0.5 * np.random.random(H))}


def reference(liq, h, x, W_in, b_in, W_v, b_v, W_o, b_o, g_att, beta_att, tau):
    liq, h = f64(liq), f64(h)
    xin = (mxq(f64(x), 1, "e4m3") @ mxq(f64(W_in), 1, "e4m3").T) + f64(b_in)
    v = (mxq(liq, 1, "e4m3") @ mxq(f64(W_v), 1, "e4m3").T) + f64(b_v)
    att = (mxq(v, 1, "e4m3") @ mxq(f64(W_o), 1, "e4m3").T) + f64(b_o)
    z = layer_norm(att + liq, f64(g_att), f64(beta_att))
    dh = (-h + np.tanh(z + xin)) / (f64(tau) + TAU_EPS)
    return h + dh

@@ -1,0 +1,300 @@
+from contextlib import ExitStack
+
+import concourse.mybir as mybir
+from concourse.masks import make_identity
+
+F32 = mybir.dt.float32
+BF16 = mybir.dt.bfloat16
+U32 = mybir.dt.uint32
+U8 = mybir.dt.uint8
+FP8X4 = mybir.dt.float8_e4m3fn_x4
+ALU = mybir.AluOpType
+ACT = mybir.ActivationFunctionType
+
+P = 128
+B, IN, H = 1024, 512, 1024
+K_PASS = 512
+BANK = 512
+CHUNK = 512
+TILES = CHUNK // P
+LN_EPS = 1e-5
+TAU_EPS = 1e-6
+SQRT_H = 32.0
+
+FLOPS = 2 * B * H * (IN + H + H)
+
+
+def tile_advancedliquidneuralnetwork_pb_kernel(
+    tc, liq, h, x, W_in, b_in, W_v, b_v, W_o, b_o, g_att, beta_att, tau, out
+):
+    nc = tc.nc
+    with ExitStack() as ctx:
+        consts = ctx.enter_context(tc.tile_pool(name="consts", bufs=1))
+        keep = ctx.enter_context(tc.tile_pool(name="keep", bufs=1))
+        raw = ctx.enter_context(tc.tile_pool(name="raw", bufs=4))
+        stage = ctx.enter_context(tc.tile_pool(name="stage", bufs=2))
+        work = ctx.enter_context(tc.tile_pool(name="work", bufs=3))
+        small = ctx.enter_context(tc.tile_pool(name="small", bufs=4))
+        psum = ctx.enter_context(tc.psum_pool(name="psum", bufs=8))
+
+        ident = consts.tile([P, P], F32)
+        make_identity(nc, ident[:])
+        ones = consts.tile([P, P], BF16)
+        nc.vector.memset(ones[:], 1.0)
+        minus_half = consts.tile([P, 1], F32)
+        nc.vector.memset(minus_half[:], -0.5)
+
+        bv = consts.tile([P, 8], BF16)
+        nc.scalar.dma_start(
+            out=bv[:].rearrange("p (c e) -> p c e", e=2),
+            in_=b_v.rearrange("(c p e) -> p c e", p=P, e=2),
+        )
+        beta_t = consts.tile([P, 8], BF16)
+        bin_t = consts.tile([P, 8], BF16)
+        with nc.allow_non_contiguous_dma(reason="two vectors of 1024, one element a partition"):
+            nc.scalar.dma_start(out=beta_t[:], in_=beta_att.rearrange("(j p) -> p j", p=P))
+            nc.scalar.dma_start(out=bin_t[:], in_=b_in.rearrange("(j p) -> p j", p=P))
+        xin_bias = consts.tile([P, 8], F32)
+        nc.vector.tensor_tensor(out=xin_bias[:], in0=beta_t[:], in1=bin_t[:], op=ALU.add)
+
+        vec_rows = consts.tile([P, 3, H], BF16)
+        nc.vector.memset(vec_rows[:], 0.0)
+        for n, vector in enumerate((b_o, g_att, tau)):
+            nc.scalar.dma_start(
+                out=vec_rows[0:1, n, :], in_=vector.rearrange("(o n) -> o n", o=1)
+            )
+
+        warm = consts.tile([P, 2], F32)
+        nc.vector.memset(warm[:], 0.0)
+        nc.scalar.activation(out=warm[:, 1:2], in_=warm[:, 0:1], func=ACT.Tanh)
+
+        liq_rows = liq.rearrange("(q p i) k -> q p i k", q=2, i=TILES)
+        h_rows = h.rearrange("(q p i) k -> q p i k", q=2, i=TILES)
+        out_rows = out.rearrange("(q p i) n -> q p i n", q=2, i=TILES)
+        wv_rows = W_v.rearrange("(g u p e) k -> g p u e k", g=2, u=2, e=2)
+        wo_rows = W_o.rearrange("(q j p) k -> q p j k", q=2, p=P)
+
+        liq_raw = [keep.tile([P, TILES, H], BF16, name="liq_raw%d" % q) for q in range(2)]
+        h_raw = [keep.tile([P, TILES, H], BF16, name="h_raw%d" % q) for q in range(2)]
+        wv_raw = [raw.tile([P, TILES, H], BF16, name="wv_raw%d" % g, tag="raw") for g in range(2)]
+        wo_raw = [raw.tile([P, TILES, H], BF16, name="wo_raw%d" % q, tag="raw") for q in range(2)]
+
+        nc.sync.dma_start(out=liq_raw[0][:], in_=liq_rows[0])
+        for g in range(2):
+            nc.sync.dma_start(
+                out=wv_raw[g][:].rearrange("p (u e) k -> p u e k", e=2), in_=wv_rows[g]
+            )
+        for q in range(2):
+            nc.sync.dma_start(out=wo_raw[q][:], in_=wo_rows[q])
+
+        bo_all = consts.tile([P, H], BF16)
+        g_all = consts.tile([P, H], BF16)
+        r_all = consts.tile([P, H], F32)
+        one_minus_r = consts.tile([P, H], F32)
+
+        def spread_vectors():
+            for half in range(2):
+                cols = slice(half * BANK, (half + 1) * BANK)
+                spread = [
+                    psum.tile([P, BANK], F32, name="spread%d" % n, tag="bank") for n in range(3)
+                ]
+                for n in range(3):
+                    nc.tensor.matmul(
+                        spread[n][:], lhsT=ones[:], rhs=vec_rows[:, n, cols], start=True, stop=True
+                    )
+                nc.scalar.copy(out=bo_all[:, cols], in_=spread[0][:])
+                nc.scalar.mul(out=g_all[:, cols], in_=spread[1][:], mul=SQRT_H)
+                nc.vector.tensor_scalar_add(out=r_all[:, cols], in0=spread[2][:], scalar1=TAU_EPS)
+            nc.vector.reciprocal(out=r_all[:], in_=r_all[:])
+            nc.gpsimd.tensor_scalar(
+                out=one_minus_r[:], in0=r_all[:], scalar1=-1.0, scalar2=1.0,
+                op0=ALU.mult, op1=ALU.add,
+            )
+
+        def mx_operand(name, passes):
+            codes = keep.tile([P, passes, 1024], U32, name=name + "_codes", align_bytes=64)
+            scales = keep.tile([P, passes, 1024], U8, name=name + "_scales", align_bytes=64)
+            return codes, scales
+
+        liq_mx = mx_operand("liq", 2)
+        wv_mx = mx_operand("wv", 2)
+        v_mx = mx_operand("v", 2)
+        wo_mx = mx_operand("wo", 2)
+        x_mx = mx_operand("x", 1)
+        win_mx = mx_operand("win", 1)
+
+        def transpose_four(word_blocks, grouped_words):
+            bank = psum.tile([P, 4, P], F32, tag="bank")
+            for n, block in enumerate(word_blocks):
+                nc.tensor.transpose(bank[:, n, :], block, ident[:])
+            nc.scalar.copy(out=grouped_words, in_=bank[:].rearrange("p (a u) r -> p a r u", u=2))
+
+        def quantise(grouped, c, operand, cols):
+            codes, scales = operand
+            nc.vector.quantize_mx(
+                out=codes[:, c, cols].bitcast(FP8X4),
+                scales=scales[:, c, cols],
+                in_=grouped[:, c, :, :].rearrange("p r t -> p (r t)"),
+            )
+
+        def prepare_k1024(rows_raw, operand, chunk):
+            words = rows_raw[:].bitcast(F32)
+            grouped = stage.tile([P, 2, CHUNK, 4], BF16, tag="staged", align_bytes=64)
+            grouped_words = grouped[:].bitcast(F32)
+            for i in range(TILES):
+                transpose_four(
+                    [words[:, i, w * P : (w + 1) * P] for w in range(4)],
+                    grouped_words[:, :, i * P : (i + 1) * P, :],
+                )
+            for c in range(2):
+                quantise(grouped, c, operand, slice(chunk * CHUNK, (chunk + 1) * CHUNK))
+
+        def prepare_k512(rows_raw, operand):
+            words = rows_raw[:].bitcast(F32)
+            grouped = stage.tile([P, 1, 1024, 4], BF16, tag="staged", align_bytes=64)
+            grouped_words = grouped[:].bitcast(F32)
+            for j in range(0, 8, 2):
+                transpose_four(
+                    [words[:, j + a, u * P : (u + 1) * P] for a in range(2) for u in range(2)],
+                    grouped_words[:, 0, j * P : (j + 2) * P, :].rearrange(
+                        "p (a r) u -> p a r u", a=2
+                    ),
+                )
+            quantise(grouped, 0, operand, slice(0, 1024))
+
+        def mx_matmul(acc, stationary, s_cols, moving, m_cols, passes):
+            for c in range(passes):
+                nc.tensor.matmul_mx(
+                    out=acc,
+                    lhsT=stationary[0][:, c, s_cols].bitcast(FP8X4),
+                    lhsT_scale=stationary[1][:, c, s_cols],
+                    rhs=moving[0][:, c, m_cols].bitcast(FP8X4),
+                    rhs_scale=moving[1][:, c, m_cols],
+                    start=(c == 0),
+                    stop=(c == passes - 1),
+                )
+
+        def tile_cols(n):
+            return slice(n * P, (n + 1) * P)
+
+        def compute_v(q):
+            grouped = stage.tile([P, 2, CHUNK, 4], BF16, tag="staged", align_bytes=64)
+            for i in range(TILES):
+                for g in range(2):
+                    bank = psum.tile([P, 4, P], F32, tag="bank")
+                    for t in range(4):
+                        mx_matmul(
+                            bank[:, t, :], wv_mx, tile_cols(4 * g + t), liq_mx,
+                            tile_cols(TILES * q + i), 2,
+                        )
+                    nc.vector.tensor_tensor(
+                        out=grouped[:, g, i * P : (i + 1) * P, :],
+                        in0=bank[:].rearrange("p t r -> p r t"),
+                        in1=bv[:, 4 * g : 4 * g + 4].unsqueeze(1).to_broadcast([P, P, 4]),
+                        op=ALU.add,
+                    )
+            for g in range(2):
+                quantise(grouped, g, v_mx, slice(q * CHUNK, (q + 1) * CHUNK))
+
+        xin_t = keep.tile([P, 8, B], F32)
+
+        def compute_xin(q):
+            cols = slice(q * CHUNK, (q + 1) * CHUNK)
+            for j in range(8):
+                bank = psum.tile([P, BANK], F32, tag="bank")
+                mx_matmul(bank[:], win_mx, tile_cols(j), x_mx, cols, 1)
+                nc.scalar.activation(
+                    out=xin_t[:, j, cols], in_=bank[:], func=ACT.Identity,
+                    bias=xin_bias[:, j : j + 1], scale=1.0,
+                )
+
+        live = {}
+
+        def layer_norm_statistics(n):
+            q, i = divmod(n, TILES)
+            residual = work.tile([P, H], F32, tag="residual")
+            nc.gpsimd.tensor_tensor(
+                out=residual[:], in0=liq_raw[q][:, i, :], in1=bo_all[:], op=ALU.add
+            )
+            u = work.tile([P, H], F32, tag="u")
+            y = work.tile([P, H], F32, tag="y", bufs=4)
+            sums = small.tile([P, 2], F32, tag="sums")
+            for half in range(2):
+                cols = slice(half * BANK, (half + 1) * BANK)
+                att = psum.tile([P, BANK], F32, tag="bank")
+                mx_matmul(att[:], v_mx, tile_cols(n), wo_mx, cols, 2)
+                nc.vector.scalar_tensor_tensor(
+                    out=u[:, cols], in0=att[:], scalar=1.0, in1=residual[:, cols],
+                    op0=ALU.mult, op1=ALU.add, accum_out=sums[:, half : half + 1],
+                )
+            minus_mean = small.tile([P, 1], F32, tag="minus_mean")
+            nc.vector.tensor_scalar(
+                out=minus_mean[:], in0=sums[:, 0:1], scalar1=sums[:, 1:2], scalar2=-1.0 / H,
+                op0=ALU.add, op1=ALU.mult,
+            )
+            square_sum = small.tile([P, 1], F32, tag="square_sum")
+            nc.scalar.activation(
+                out=y[:], in_=u[:], func=ACT.Square, bias=minus_mean[:], scale=1.0,
+                accum_out=square_sum[:],
+            )
+            rstd = small.tile([P, 1], F32, tag="rstd")
+            nc.gpsimd.tensor_scalar_add(out=rstd[:], in0=square_sum[:], scalar1=H * LN_EPS)
+            nc.gpsimd.tensor_tensor(out=rstd[:], in0=rstd[:], in1=minus_half[:], op=ALU.pow)
+            live[n] = (u, y, minus_mean, rstd)
+
+        def finish(n):
+            q, i = divmod(n, TILES)
+            u, y, minus_mean, rstd = live[n]
+            kept = work.tile([P, H], F32, tag="kept")
+            nc.gpsimd.tensor_tensor(
+                out=kept[:], in0=h_raw[q][:, i, :], in1=one_minus_r[:], op=ALU.mult
+            )
+            xin = [psum.tile([P, 4, P], F32, name="xin%d" % half, tag="bank") for half in range(2)]
+            for j in range(8):
+                nc.tensor.transpose(xin[j // 4][:, j % 4, :], xin_t[:, j, tile_cols(n)], ident[:])
+            nc.vector.scalar_tensor_tensor(
+                out=y[:], in0=u[:], scalar=minus_mean[:], in1=g_all[:], op0=ALU.add, op1=ALU.mult
+            )
+            for half in range(2):
+                cols = slice(half * BANK, (half + 1) * BANK)
+                nc.vector.scalar_tensor_tensor(
+                    out=y[:, cols], in0=y[:, cols], scalar=rstd[:],
+                    in1=xin[half][:].rearrange("p a r -> p (a r)"), op0=ALU.mult, op1=ALU.add,
+                )
+            nc.scalar.activation(out=y[:], in_=y[:], func=ACT.Tanh)
+            nc.vector.tensor_tensor(out=y[:], in0=y[:], in1=r_all[:], op=ALU.mult)
+            nc.gpsimd.tensor_tensor(out=y[:], in0=y[:], in1=kept[:], op=ALU.add)
+            nc.sync.dma_start(out=out_rows[q][:, i, :], in_=y[:])
+
+        prepare_k1024(liq_raw[0], liq_mx, 0)
+        for g in range(2):
+            prepare_k1024(wv_raw[g], wv_mx, g)
+        spread_vectors()
+
+        win_raw = raw.tile([P, 8, IN], BF16, tag="raw")
+        x_raw = raw.tile([P, 8, IN], BF16, tag="raw")
+        nc.sync.dma_start(out=win_raw[:], in_=W_in.rearrange("(j p) k -> p j k", p=P))
+        nc.sync.dma_start(
+            out=x_raw[:].rearrange("p (q i) k -> p q i k", q=2),
+            in_=x.rearrange("(q p i) k -> p q i k", q=2, i=TILES),
+        )
+        nc.sync.dma_start(out=liq_raw[1][:], in_=liq_rows[1])
+        for q in range(2):
+            nc.sync.dma_start(out=h_raw[q][:], in_=h_rows[q])
+
+        compute_v(0)
+        for q in range(2):
+            prepare_k1024(wo_raw[q], wo_mx, q)
+        layer_norm_statistics(0)
+        prepare_k512(win_raw, win_mx)
+        prepare_k512(x_raw, x_mx)
+        compute_xin(0)
+        layer_norm_statistics(1)
+        finish(0)
+        prepare_k1024(liq_raw[1], liq_mx, 1)
+        compute_v(1)
+        compute_xin(1)
+        for n in range(2, 8):
+            layer_norm_statistics(n)
+            finish(n - 1)
+        finish(7)

@@ -57,7 +57,7 @@ def tile_advancedliquidneuralnetwork_pb_kernel(
         xin_bias = consts.tile([P, 8], F32)
         nc.vector.tensor_tensor(out=xin_bias[:], in0=beta_t[:], in1=bin_t[:], op=ALU.add)
 
-        vec_rows = consts.tile([P, 3, H], BF16)
+        vec_rows = stage.tile([P, 3, H], BF16, tag="staged", align_bytes=64)
         nc.vector.memset(vec_rows[:], 0.0)
         for n, vector in enumerate((b_o, g_att, tau)):
             nc.scalar.dma_start(
@@ -75,7 +75,6 @@ def tile_advancedliquidneuralnetwork_pb_kernel(
         wo_rows = W_o.rearrange("(q j p) k -> q p j k", q=2, p=P)
 
         liq_raw = [keep.tile([P, TILES, H], BF16, name="liq_raw%d" % q) for q in range(2)]
-        h_raw = [keep.tile([P, TILES, H], BF16, name="h_raw%d" % q) for q in range(2)]
         wv_raw = [raw.tile([P, TILES, H], BF16, name="wv_raw%d" % g, tag="raw") for g in range(2)]
         wo_raw = [raw.tile([P, TILES, H], BF16, name="wo_raw%d" % q, tag="raw") for q in range(2)]
 
@@ -84,6 +83,7 @@ def tile_advancedliquidneuralnetwork_pb_kernel(
             nc.sync.dma_start(
                 out=wv_raw[g][:].rearrange("p (u e) k -> p u e k", e=2), in_=wv_rows[g]
             )
+        nc.sync.dma_start(out=liq_raw[1][:], in_=liq_rows[1])
         for q in range(2):
             nc.sync.dma_start(out=wo_raw[q][:], in_=wo_rows[q])
 
@@ -208,15 +208,17 @@ def tile_advancedliquidneuralnetwork_pb_kernel(
                     bias=xin_bias[:, j : j + 1], scale=1.0,
                 )
 
-        live = {}
+        residual, u_of, y_of, minus_mean_of, rstd_of, kept_of = {}, {}, {}, {}, {}, {}
 
-        def layer_norm_statistics(n):
+        def add_bias_to_liq(n):
             q, i = divmod(n, TILES)
-            residual = work.tile([P, H], F32, tag="residual")
+            residual[n] = work.tile([P, H], F32, name="residual", tag="residual", bufs=8)
             nc.gpsimd.tensor_tensor(
-                out=residual[:], in0=liq_raw[q][:, i, :], in1=bo_all[:], op=ALU.add
+                out=residual[n][:], in0=liq_raw[q][:, i, :], in1=bo_all[:], op=ALU.add
             )
-            u = work.tile([P, H], F32, tag="u")
+
+        def statistics(n):
+            u = work.tile([P, H], F32, tag="u", bufs=2)
             y = work.tile([P, H], F32, tag="y", bufs=4)
             sums = small.tile([P, 2], F32, tag="sums")
             for half in range(2):
@@ -224,7 +226,7 @@ def tile_advancedliquidneuralnetwork_pb_kernel(
                 att = psum.tile([P, BANK], F32, tag="bank")
                 mx_matmul(att[:], v_mx, tile_cols(n), wo_mx, cols, 2)
                 nc.vector.scalar_tensor_tensor(
-                    out=u[:, cols], in0=att[:], scalar=1.0, in1=residual[:, cols],
+                    out=u[:, cols], in0=att[:], scalar=1.0, in1=residual[n][:, cols],
                     op0=ALU.mult, op1=ALU.add, accum_out=sums[:, half : half + 1],
                 )
             minus_mean = small.tile([P, 1], F32, tag="minus_mean")
@@ -240,36 +242,44 @@ def tile_advancedliquidneuralnetwork_pb_kernel(
             rstd = small.tile([P, 1], F32, tag="rstd")
             nc.gpsimd.tensor_scalar_add(out=rstd[:], in0=square_sum[:], scalar1=H * LN_EPS)
             nc.gpsimd.tensor_tensor(out=rstd[:], in0=rstd[:], in1=minus_half[:], op=ALU.pow)
-            live[n] = (u, y, minus_mean, rstd)
+            u_of[n], y_of[n], minus_mean_of[n], rstd_of[n] = u, y, minus_mean, rstd
 
-        def finish(n):
+        def tanh_argument(n):
             q, i = divmod(n, TILES)
-            u, y, minus_mean, rstd = live[n]
-            kept = work.tile([P, H], F32, tag="kept")
+            u, y = u_of[n], y_of[n]
+            kept_of[n] = work.tile([P, H], F32, name="kept", tag="kept", bufs=2)
             nc.gpsimd.tensor_tensor(
-                out=kept[:], in0=h_raw[q][:, i, :], in1=one_minus_r[:], op=ALU.mult
+                out=kept_of[n][:], in0=h_raw[q][:, i, :], in1=one_minus_r[:], op=ALU.mult
             )
             xin = [psum.tile([P, 4, P], F32, name="xin%d" % half, tag="bank") for half in range(2)]
             for j in range(8):
                 nc.tensor.transpose(xin[j // 4][:, j % 4, :], xin_t[:, j, tile_cols(n)], ident[:])
             nc.vector.scalar_tensor_tensor(
-                out=y[:], in0=u[:], scalar=minus_mean[:], in1=g_all[:], op0=ALU.add, op1=ALU.mult
+                out=y[:], in0=u[:], scalar=minus_mean_of[n][:], in1=g_all[:],
+                op0=ALU.add, op1=ALU.mult,
             )
             for half in range(2):
                 cols = slice(half * BANK, (half + 1) * BANK)
                 nc.vector.scalar_tensor_tensor(
-                    out=y[:, cols], in0=y[:, cols], scalar=rstd[:],
+                    out=y[:, cols], in0=y[:, cols], scalar=rstd_of[n][:],
                     in1=xin[half][:].rearrange("p a r -> p (a r)"), op0=ALU.mult, op1=ALU.add,
                 )
             nc.scalar.activation(out=y[:], in_=y[:], func=ACT.Tanh)
+
+        def update(n):
+            q, i = divmod(n, TILES)
+            y = y_of[n]
             nc.vector.tensor_tensor(out=y[:], in0=y[:], in1=r_all[:], op=ALU.mult)
-            nc.gpsimd.tensor_tensor(out=y[:], in0=y[:], in1=kept[:], op=ALU.add)
+            nc.vector.tensor_tensor(out=y[:], in0=y[:], in1=kept_of[n][:], op=ALU.add)
             nc.sync.dma_start(out=out_rows[q][:, i, :], in_=y[:])
 
         prepare_k1024(liq_raw[0], liq_mx, 0)
+        spread_vectors()
         for g in range(2):
             prepare_k1024(wv_raw[g], wv_mx, g)
-        spread_vectors()
+        prepare_k1024(liq_raw[1], liq_mx, 1)
+        for n in range(8):
+            add_bias_to_liq(n)
 
         win_raw = raw.tile([P, 8, IN], BF16, tag="raw")
         x_raw = raw.tile([P, 8, IN], BF16, tag="raw")
@@ -278,23 +288,24 @@ def tile_advancedliquidneuralnetwork_pb_kernel(
             out=x_raw[:].rearrange("p (q i) k -> p q i k", q=2),
             in_=x.rearrange("(q p i) k -> p q i k", q=2, i=TILES),
         )
-        nc.sync.dma_start(out=liq_raw[1][:], in_=liq_rows[1])
-        for q in range(2):
-            nc.sync.dma_start(out=h_raw[q][:], in_=h_rows[q])
-
         compute_v(0)
         for q in range(2):
             prepare_k1024(wo_raw[q], wo_mx, q)
-        layer_norm_statistics(0)
+        h_raw = [raw.tile([P, TILES, H], BF16, name="h_raw%d" % q, tag="raw") for q in range(2)]
+        for q in range(2):
+            nc.sync.dma_start(out=h_raw[q][:], in_=h_rows[q])
+        compute_v(1)
+        statistics(0)
         prepare_k512(win_raw, win_mx)
         prepare_k512(x_raw, x_mx)
         compute_xin(0)
-        layer_norm_statistics(1)
-        finish(0)
-        prepare_k1024(liq_raw[1], liq_mx, 1)
-        compute_v(1)
         compute_xin(1)
+        statistics(1)
+        tanh_argument(0)
         for n in range(2, 8):
-            layer_norm_statistics(n)
-            finish(n - 1)
-        finish(7)
+            statistics(n)
+            tanh_argument(n - 1)
+            update(n - 2)
+        tanh_argument(7)
+        update(6)
+        update(7)

@@ -20,6 +20,7 @@ TILES = CHUNK // P
 LN_EPS = 1e-5
 TAU_EPS = 1e-6
 SQRT_H = 32.0
+GPSIMD_COLS = 256
 
 FLOPS = 2 * B * H * (IN + H + H)
 
@@ -208,14 +209,17 @@ def tile_advancedliquidneuralnetwork_pb_kernel(
                     bias=xin_bias[:, j : j + 1], scale=1.0,
                 )
 
+        gpsimd_pieces = [slice(c, c + GPSIMD_COLS) for c in range(0, H, GPSIMD_COLS)]
         residual, u_of, y_of, minus_mean_of, rstd_of, kept_of = {}, {}, {}, {}, {}, {}
 
         def add_bias_to_liq(n):
             q, i = divmod(n, TILES)
             residual[n] = work.tile([P, H], F32, name="residual", tag="residual", bufs=8)
-            nc.gpsimd.tensor_tensor(
-                out=residual[n][:], in0=liq_raw[q][:, i, :], in1=bo_all[:], op=ALU.add
-            )
+            for cols in gpsimd_pieces:
+                nc.gpsimd.tensor_tensor(
+                    out=residual[n][:, cols], in0=liq_raw[q][:, i, cols], in1=bo_all[:, cols],
+                    op=ALU.add,
+                )
 
         def statistics(n):
             u = work.tile([P, H], F32, tag="u", bufs=2)
@@ -248,9 +252,11 @@ def tile_advancedliquidneuralnetwork_pb_kernel(
             q, i = divmod(n, TILES)
             u, y = u_of[n], y_of[n]
             kept_of[n] = work.tile([P, H], F32, name="kept", tag="kept", bufs=2)
-            nc.gpsimd.tensor_tensor(
-                out=kept_of[n][:], in0=h_raw[q][:, i, :], in1=one_minus_r[:], op=ALU.mult
-            )
+            for cols in gpsimd_pieces:
+                nc.gpsimd.tensor_tensor(
+                    out=kept_of[n][:, cols], in0=h_raw[q][:, i, cols], in1=one_minus_r[:, cols],
+                    op=ALU.mult,
+                )
             xin = [psum.tile([P, 4, P], F32, name="xin%d" % half, tag="bank") for half in range(2)]
             for j in range(8):
                 nc.tensor.transpose(xin[j // 4][:, j % 4, :], xin_t[:, j, tile_cols(n)], ident[:])

@@ -20,7 +20,6 @@ TILES = CHUNK // P
 LN_EPS = 1e-5
 TAU_EPS = 1e-6
 SQRT_H = 32.0
-GPSIMD_COLS = 256
 
 FLOPS = 2 * B * H * (IN + H + H)
 
@@ -209,17 +208,14 @@ def tile_advancedliquidneuralnetwork_pb_kernel(
                     bias=xin_bias[:, j : j + 1], scale=1.0,
                 )
 
-        gpsimd_pieces = [slice(c, c + GPSIMD_COLS) for c in range(0, H, GPSIMD_COLS)]
         residual, u_of, y_of, minus_mean_of, rstd_of, kept_of = {}, {}, {}, {}, {}, {}
 
         def add_bias_to_liq(n):
             q, i = divmod(n, TILES)
-            residual[n] = work.tile([P, H], F32, name="residual", tag="residual", bufs=8)
-            for cols in gpsimd_pieces:
-                nc.gpsimd.tensor_tensor(
-                    out=residual[n][:, cols], in0=liq_raw[q][:, i, cols], in1=bo_all[:, cols],
-                    op=ALU.add,
-                )
+            residual[n] = work.tile([P, H], F32, name="residual", tag="residual", bufs=2)
+            nc.vector.tensor_tensor(
+                out=residual[n][:], in0=liq_raw[q][:, i, :], in1=bo_all[:], op=ALU.add
+            )
 
         def statistics(n):
             u = work.tile([P, H], F32, tag="u", bufs=2)
@@ -252,11 +248,9 @@ def tile_advancedliquidneuralnetwork_pb_kernel(
             q, i = divmod(n, TILES)
             u, y = u_of[n], y_of[n]
             kept_of[n] = work.tile([P, H], F32, name="kept", tag="kept", bufs=2)
-            for cols in gpsimd_pieces:
-                nc.gpsimd.tensor_tensor(
-                    out=kept_of[n][:, cols], in0=h_raw[q][:, i, cols], in1=one_minus_r[:, cols],
-                    op=ALU.mult,
-                )
+            nc.gpsimd.tensor_tensor(
+                out=kept_of[n][:], in0=h_raw[q][:, i, :], in1=one_minus_r[:], op=ALU.mult
+            )
             xin = [psum.tile([P, 4, P], F32, name="xin%d" % half, tag="bank") for half in range(2)]
             for j in range(8):
                 nc.tensor.transpose(xin[j // 4][:, j % 4, :], xin_t[:, j, tile_cols(n)], ident[:])
@@ -284,8 +278,6 @@ def tile_advancedliquidneuralnetwork_pb_kernel(
         for g in range(2):
             prepare_k1024(wv_raw[g], wv_mx, g)
         prepare_k1024(liq_raw[1], liq_mx, 1)
-        for n in range(8):
-            add_bias_to_liq(n)
 
         win_raw = raw.tile([P, 8, IN], BF16, tag="raw")
         x_raw = raw.tile([P, 8, IN], BF16, tag="raw")
@@ -301,15 +293,20 @@ def tile_advancedliquidneuralnetwork_pb_kernel(
         for q in range(2):
             nc.sync.dma_start(out=h_raw[q][:], in_=h_rows[q])
         compute_v(1)
+        add_bias_to_liq(0)
         statistics(0)
+        add_bias_to_liq(1)
         prepare_k512(win_raw, win_mx)
         prepare_k512(x_raw, x_mx)
         compute_xin(0)
         compute_xin(1)
         statistics(1)
+        add_bias_to_liq(2)
         tanh_argument(0)
         for n in range(2, 8):
             statistics(n)
+            if n + 1 < 8:
+                add_bias_to_liq(n + 1)
             tanh_argument(n - 1)
             update(n - 2)
         tanh_argument(7)

@@ -51,15 +51,19 @@ def tile_advancedliquidneuralnetwork_pb_kernel(
         )
         beta_t = consts.tile([P, 8], BF16)
         bin_t = consts.tile([P, 8], BF16)
-        with nc.allow_non_contiguous_dma(reason="two vectors of 1024, one element a partition"):
+        bo_t = consts.tile([P, 8], BF16)
+        with nc.allow_non_contiguous_dma(reason="three vectors of 1024, one element a partition"):
             nc.scalar.dma_start(out=beta_t[:], in_=beta_att.rearrange("(j p) -> p j", p=P))
             nc.scalar.dma_start(out=bin_t[:], in_=b_in.rearrange("(j p) -> p j", p=P))
+            nc.scalar.dma_start(out=bo_t[:], in_=b_o.rearrange("(j p) -> p j", p=P))
         xin_bias = consts.tile([P, 8], F32)
         nc.vector.tensor_tensor(out=xin_bias[:], in0=beta_t[:], in1=bin_t[:], op=ALU.add)
+        att_bias = consts.tile([P, 8], F32)
+        nc.vector.tensor_copy(out=att_bias[:], in_=bo_t[:])
 
-        vec_rows = stage.tile([P, 3, H], BF16, tag="staged", align_bytes=64)
+        vec_rows = stage.tile([P, 2, H], BF16, tag="staged", align_bytes=64)
         nc.vector.memset(vec_rows[:], 0.0)
-        for n, vector in enumerate((b_o, g_att, tau)):
+        for n, vector in enumerate((g_att, tau)):
             nc.scalar.dma_start(
                 out=vec_rows[0:1, n, :], in_=vector.rearrange("(o n) -> o n", o=1)
             )
@@ -87,7 +91,6 @@ def tile_advancedliquidneuralnetwork_pb_kernel(
         for q in range(2):
             nc.sync.dma_start(out=wo_raw[q][:], in_=wo_rows[q])
 
-        bo_all = consts.tile([P, H], BF16)
         g_all = consts.tile([P, H], BF16)
         r_all = consts.tile([P, H], F32)
         one_minus_r = consts.tile([P, H], F32)
@@ -96,15 +99,14 @@ def tile_advancedliquidneuralnetwork_pb_kernel(
             for half in range(2):
                 cols = slice(half * BANK, (half + 1) * BANK)
                 spread = [
-                    psum.tile([P, BANK], F32, name="spread%d" % n, tag="bank") for n in range(3)
+                    psum.tile([P, BANK], F32, name="spread%d" % n, tag="bank") for n in range(2)
                 ]
-                for n in range(3):
+                for n in range(2):
                     nc.tensor.matmul(
                         spread[n][:], lhsT=ones[:], rhs=vec_rows[:, n, cols], start=True, stop=True
                     )
-                nc.scalar.copy(out=bo_all[:, cols], in_=spread[0][:])
-                nc.scalar.mul(out=g_all[:, cols], in_=spread[1][:], mul=SQRT_H)
-                nc.vector.tensor_scalar_add(out=r_all[:, cols], in0=spread[2][:], scalar1=TAU_EPS)
+                nc.scalar.mul(out=g_all[:, cols], in_=spread[0][:], mul=SQRT_H)
+                nc.vector.tensor_scalar_add(out=r_all[:, cols], in0=spread[1][:], scalar1=TAU_EPS)
             nc.vector.reciprocal(out=r_all[:], in_=r_all[:])
             nc.gpsimd.tensor_scalar(
                 out=one_minus_r[:], in0=r_all[:], scalar1=-1.0, scalar2=1.0,
@@ -197,37 +199,37 @@ def tile_advancedliquidneuralnetwork_pb_kernel(
                 quantise(grouped, g, v_mx, slice(q * CHUNK, (q + 1) * CHUNK))
 
         xin_t = keep.tile([P, 8, B], F32)
+        att_t = keep.tile([P, 8, B], F32)
 
-        def compute_xin(q):
+        def feature_major(dest, weights, moving, passes, bias, q):
             cols = slice(q * CHUNK, (q + 1) * CHUNK)
             for j in range(8):
                 bank = psum.tile([P, BANK], F32, tag="bank")
-                mx_matmul(bank[:], win_mx, tile_cols(j), x_mx, cols, 1)
+                mx_matmul(bank[:], weights, tile_cols(j), moving, cols, passes)
                 nc.scalar.activation(
-                    out=xin_t[:, j, cols], in_=bank[:], func=ACT.Identity,
-                    bias=xin_bias[:, j : j + 1], scale=1.0,
+                    out=dest[:, j, cols], in_=bank[:], func=ACT.Identity,
+                    bias=bias[:, j : j + 1], scale=1.0,
                 )
 
-        residual, u_of, y_of, minus_mean_of, rstd_of, kept_of = {}, {}, {}, {}, {}, {}
+        def batch_major(source, n):
+            halves = [psum.tile([P, 4, P], F32, name="half%d" % k, tag="bank") for k in range(2)]
+            for j in range(8):
+                nc.tensor.transpose(halves[j // 4][:, j % 4, :], source[:, j, tile_cols(n)], ident[:])
+            return [half[:].rearrange("p a r -> p (a r)") for half in halves]
 
-        def add_bias_to_liq(n):
-            q, i = divmod(n, TILES)
-            residual[n] = work.tile([P, H], F32, name="residual", tag="residual", bufs=2)
-            nc.vector.tensor_tensor(
-                out=residual[n][:], in0=liq_raw[q][:, i, :], in1=bo_all[:], op=ALU.add
-            )
+        u_of, y_of, minus_mean_of, rstd_of, kept_of = {}, {}, {}, {}, {}
+        bank_cols = [slice(k * BANK, (k + 1) * BANK) for k in range(2)]
 
         def statistics(n):
+            q, i = divmod(n, TILES)
             u = work.tile([P, H], F32, tag="u", bufs=2)
             y = work.tile([P, H], F32, tag="y", bufs=4)
             sums = small.tile([P, 2], F32, tag="sums")
-            for half in range(2):
-                cols = slice(half * BANK, (half + 1) * BANK)
-                att = psum.tile([P, BANK], F32, tag="bank")
-                mx_matmul(att[:], v_mx, tile_cols(n), wo_mx, cols, 2)
+            att = batch_major(att_t, n)
+            for k, cols in enumerate(bank_cols):
                 nc.vector.scalar_tensor_tensor(
-                    out=u[:, cols], in0=att[:], scalar=1.0, in1=residual[n][:, cols],
-                    op0=ALU.mult, op1=ALU.add, accum_out=sums[:, half : half + 1],
+                    out=u[:, cols], in0=att[k], scalar=1.0, in1=liq_raw[q][:, i, cols],
+                    op0=ALU.mult, op1=ALU.add, accum_out=sums[:, k : k + 1],
                 )
             minus_mean = small.tile([P, 1], F32, tag="minus_mean")
             nc.vector.tensor_scalar(
@@ -244,34 +246,47 @@ def tile_advancedliquidneuralnetwork_pb_kernel(
             nc.gpsimd.tensor_tensor(out=rstd[:], in0=rstd[:], in1=minus_half[:], op=ALU.pow)
             u_of[n], y_of[n], minus_mean_of[n], rstd_of[n] = u, y, minus_mean, rstd
 
-        def tanh_argument(n):
+        def centre_and_scale(n):
             q, i = divmod(n, TILES)
-            u, y = u_of[n], y_of[n]
             kept_of[n] = work.tile([P, H], F32, name="kept", tag="kept", bufs=2)
             nc.gpsimd.tensor_tensor(
                 out=kept_of[n][:], in0=h_raw[q][:, i, :], in1=one_minus_r[:], op=ALU.mult
             )
-            xin = [psum.tile([P, 4, P], F32, name="xin%d" % half, tag="bank") for half in range(2)]
-            for j in range(8):
-                nc.tensor.transpose(xin[j // 4][:, j % 4, :], xin_t[:, j, tile_cols(n)], ident[:])
             nc.vector.scalar_tensor_tensor(
-                out=y[:], in0=u[:], scalar=minus_mean_of[n][:], in1=g_all[:],
+                out=y_of[n][:], in0=u_of[n][:], scalar=minus_mean_of[n][:], in1=g_all[:],
                 op0=ALU.add, op1=ALU.mult,
             )
-            for half in range(2):
-                cols = slice(half * BANK, (half + 1) * BANK)
+
+        def add_xin_and_tanh(n):
+            y = y_of[n]
+            xin = batch_major(xin_t, n)
+            for k, cols in enumerate(bank_cols):
                 nc.vector.scalar_tensor_tensor(
-                    out=y[:, cols], in0=y[:, cols], scalar=rstd_of[n][:],
-                    in1=xin[half][:].rearrange("p a r -> p (a r)"), op0=ALU.mult, op1=ALU.add,
+                    out=y[:, cols], in0=y[:, cols], scalar=rstd_of[n][:], in1=xin[k],
+                    op0=ALU.mult, op1=ALU.add,
                 )
             nc.scalar.activation(out=y[:], in_=y[:], func=ACT.Tanh)
 
-        def update(n):
+        def times_r(n):
+            nc.vector.tensor_tensor(out=y_of[n][:], in0=y_of[n][:], in1=r_all[:], op=ALU.mult)
+
+        def add_kept_and_store(n):
             q, i = divmod(n, TILES)
             y = y_of[n]
-            nc.vector.tensor_tensor(out=y[:], in0=y[:], in1=r_all[:], op=ALU.mult)
             nc.vector.tensor_tensor(out=y[:], in0=y[:], in1=kept_of[n][:], op=ALU.add)
             nc.sync.dma_start(out=out_rows[q][:, i, :], in_=y[:])
+
+        def step(n):
+            if n < 8:
+                statistics(n)
+            if 0 <= n - 1 < 8:
+                centre_and_scale(n - 1)
+            if 0 <= n - 2 < 8:
+                times_r(n - 2)
+            if 0 <= n - 1 < 8:
+                add_xin_and_tanh(n - 1)
+            if 0 <= n - 2 < 8:
+                add_kept_and_store(n - 2)
 
         prepare_k1024(liq_raw[0], liq_mx, 0)
         spread_vectors()
@@ -292,23 +307,14 @@ def tile_advancedliquidneuralnetwork_pb_kernel(
         h_raw = [raw.tile([P, TILES, H], BF16, name="h_raw%d" % q, tag="raw") for q in range(2)]
         for q in range(2):
             nc.sync.dma_start(out=h_raw[q][:], in_=h_rows[q])
+        feature_major(att_t, wo_mx, v_mx, 2, att_bias, 0)
         compute_v(1)
-        add_bias_to_liq(0)
-        statistics(0)
-        add_bias_to_liq(1)
+        step(0)
         prepare_k512(win_raw, win_mx)
         prepare_k512(x_raw, x_mx)
-        compute_xin(0)
-        compute_xin(1)
-        statistics(1)
-        add_bias_to_liq(2)
-        tanh_argument(0)
-        for n in range(2, 8):
-            statistics(n)
-            if n + 1 < 8:
-                add_bias_to_liq(n + 1)
-            tanh_argument(n - 1)
-            update(n - 2)
-        tanh_argument(7)
-        update(6)
-        update(7)
+        feature_major(xin_t, win_mx, x_mx, 1, xin_bias, 0)
+        step(1)
+        feature_major(att_t, wo_mx, v_mx, 2, att_bias, 1)
+        feature_major(xin_t, win_mx, x_mx, 1, xin_bias, 1)
+        for n in range(2, 10):
+            step(n)

@@ -49,21 +49,10 @@ def tile_advancedliquidneuralnetwork_pb_kernel(
             out=bv[:].rearrange("p (c e) -> p c e", e=2),
             in_=b_v.rearrange("(c p e) -> p c e", p=P, e=2),
         )
-        beta_t = consts.tile([P, 8], BF16)
-        bin_t = consts.tile([P, 8], BF16)
-        bo_t = consts.tile([P, 8], BF16)
-        with nc.allow_non_contiguous_dma(reason="three vectors of 1024, one element a partition"):
-            nc.scalar.dma_start(out=beta_t[:], in_=beta_att.rearrange("(j p) -> p j", p=P))
-            nc.scalar.dma_start(out=bin_t[:], in_=b_in.rearrange("(j p) -> p j", p=P))
-            nc.scalar.dma_start(out=bo_t[:], in_=b_o.rearrange("(j p) -> p j", p=P))
-        xin_bias = consts.tile([P, 8], F32)
-        nc.vector.tensor_tensor(out=xin_bias[:], in0=beta_t[:], in1=bin_t[:], op=ALU.add)
-        att_bias = consts.tile([P, 8], F32)
-        nc.vector.tensor_copy(out=att_bias[:], in_=bo_t[:])
 
-        vec_rows = stage.tile([P, 2, H], BF16, tag="staged", align_bytes=64)
+        vec_rows = stage.tile([P, 3, H], BF16, tag="staged", align_bytes=64)
         nc.vector.memset(vec_rows[:], 0.0)
-        for n, vector in enumerate((g_att, tau)):
+        for n, vector in enumerate((b_o, g_att, tau)):
             nc.scalar.dma_start(
                 out=vec_rows[0:1, n, :], in_=vector.rearrange("(o n) -> o n", o=1)
             )
@@ -81,16 +70,16 @@ def tile_advancedliquidneuralnetwork_pb_kernel(
         liq_raw = [keep.tile([P, TILES, H], BF16, name="liq_raw%d" % q) for q in range(2)]
         wv_raw = [raw.tile([P, TILES, H], BF16, name="wv_raw%d" % g, tag="raw") for g in range(2)]
         wo_raw = [raw.tile([P, TILES, H], BF16, name="wo_raw%d" % q, tag="raw") for q in range(2)]
-
-        nc.sync.dma_start(out=liq_raw[0][:], in_=liq_rows[0])
+        for q in range(2):
+            nc.sync.dma_start(out=liq_raw[q][:], in_=liq_rows[q])
         for g in range(2):
             nc.sync.dma_start(
                 out=wv_raw[g][:].rearrange("p (u e) k -> p u e k", e=2), in_=wv_rows[g]
             )
-        nc.sync.dma_start(out=liq_raw[1][:], in_=liq_rows[1])
         for q in range(2):
             nc.sync.dma_start(out=wo_raw[q][:], in_=wo_rows[q])
 
+        bo_all = consts.tile([P, H], BF16)
         g_all = consts.tile([P, H], BF16)
         r_all = consts.tile([P, H], F32)
         one_minus_r = consts.tile([P, H], F32)
@@ -99,14 +88,15 @@ def tile_advancedliquidneuralnetwork_pb_kernel(
             for half in range(2):
                 cols = slice(half * BANK, (half + 1) * BANK)
                 spread = [
-                    psum.tile([P, BANK], F32, name="spread%d" % n, tag="bank") for n in range(2)
+                    psum.tile([P, BANK], F32, name="spread%d" % n, tag="bank") for n in range(3)
                 ]
-                for n in range(2):
+                for n in range(3):
                     nc.tensor.matmul(
                         spread[n][:], lhsT=ones[:], rhs=vec_rows[:, n, cols], start=True, stop=True
                     )
-                nc.scalar.mul(out=g_all[:, cols], in_=spread[0][:], mul=SQRT_H)
-                nc.vector.tensor_scalar_add(out=r_all[:, cols], in0=spread[1][:], scalar1=TAU_EPS)
+                nc.scalar.copy(out=bo_all[:, cols], in_=spread[0][:])
+                nc.scalar.mul(out=g_all[:, cols], in_=spread[1][:], mul=SQRT_H)
+                nc.vector.tensor_scalar_add(out=r_all[:, cols], in0=spread[2][:], scalar1=TAU_EPS)
             nc.vector.reciprocal(out=r_all[:], in_=r_all[:])
             nc.gpsimd.tensor_scalar(
                 out=one_minus_r[:], in0=r_all[:], scalar1=-1.0, scalar2=1.0,
@@ -179,56 +169,53 @@ def tile_advancedliquidneuralnetwork_pb_kernel(
         def tile_cols(n):
             return slice(n * P, (n + 1) * P)
 
-        def compute_v(q):
-            grouped = stage.tile([P, 2, CHUNK, 4], BF16, tag="staged", align_bytes=64)
-            for i in range(TILES):
-                for g in range(2):
-                    bank = psum.tile([P, 4, P], F32, tag="bank")
-                    for t in range(4):
-                        mx_matmul(
-                            bank[:, t, :], wv_mx, tile_cols(4 * g + t), liq_mx,
-                            tile_cols(TILES * q + i), 2,
-                        )
-                    nc.vector.tensor_tensor(
-                        out=grouped[:, g, i * P : (i + 1) * P, :],
-                        in0=bank[:].rearrange("p t r -> p r t"),
-                        in1=bv[:, 4 * g : 4 * g + 4].unsqueeze(1).to_broadcast([P, P, 4]),
-                        op=ALU.add,
-                    )
+        def compute_v(n):
+            grouped = stage.tile([P, 2, P, 4], BF16, tag="v_grouped", bufs=3, align_bytes=64)
             for g in range(2):
-                quantise(grouped, g, v_mx, slice(q * CHUNK, (q + 1) * CHUNK))
+                bank = psum.tile([P, 4, P], F32, tag="bank")
+                for t in range(4):
+                    mx_matmul(bank[:, t, :], wv_mx, tile_cols(4 * g + t), liq_mx, tile_cols(n), 2)
+                nc.vector.tensor_tensor(
+                    out=grouped[:, g, :, :],
+                    in0=bank[:].rearrange("p t r -> p r t"),
+                    in1=bv[:, 4 * g : 4 * g + 4].unsqueeze(1).to_broadcast([P, P, 4]),
+                    op=ALU.add,
+                )
+            for g in range(2):
+                quantise(grouped, g, v_mx, tile_cols(n))
 
         xin_t = keep.tile([P, 8, B], F32)
-        att_t = keep.tile([P, 8, B], F32)
+        xin_bias = consts.tile([P, 8], F32)
 
-        def feature_major(dest, weights, moving, passes, bias, q):
+        def compute_xin(q, features):
             cols = slice(q * CHUNK, (q + 1) * CHUNK)
-            for j in range(8):
+            for j in features:
                 bank = psum.tile([P, BANK], F32, tag="bank")
-                mx_matmul(bank[:], weights, tile_cols(j), moving, cols, passes)
+                mx_matmul(bank[:], win_mx, tile_cols(j), x_mx, cols, 1)
                 nc.scalar.activation(
-                    out=dest[:, j, cols], in_=bank[:], func=ACT.Identity,
-                    bias=bias[:, j : j + 1], scale=1.0,
+                    out=xin_t[:, j, cols], in_=bank[:], func=ACT.Identity,
+                    bias=xin_bias[:, j : j + 1], scale=1.0,
                 )
 
-        def batch_major(source, n):
-            halves = [psum.tile([P, 4, P], F32, name="half%d" % k, tag="bank") for k in range(2)]
-            for j in range(8):
-                nc.tensor.transpose(halves[j // 4][:, j % 4, :], source[:, j, tile_cols(n)], ident[:])
-            return [half[:].rearrange("p a r -> p (a r)") for half in halves]
-
-        u_of, y_of, minus_mean_of, rstd_of, kept_of = {}, {}, {}, {}, {}
+        residual, u_of, y_of, minus_mean_of, rstd_of, kept_of = {}, {}, {}, {}, {}, {}
         bank_cols = [slice(k * BANK, (k + 1) * BANK) for k in range(2)]
 
-        def statistics(n):
+        def add_bias_to_liq(n):
             q, i = divmod(n, TILES)
+            residual[n] = work.tile([P, H], F32, name="residual", tag="residual", bufs=8)
+            nc.gpsimd.tensor_tensor(
+                out=residual[n][:], in0=liq_raw[q][:, i, :], in1=bo_all[:], op=ALU.add
+            )
+
+        def statistics(n):
             u = work.tile([P, H], F32, tag="u", bufs=2)
             y = work.tile([P, H], F32, tag="y", bufs=4)
             sums = small.tile([P, 2], F32, tag="sums")
-            att = batch_major(att_t, n)
             for k, cols in enumerate(bank_cols):
+                att = psum.tile([P, BANK], F32, tag="bank")
+                mx_matmul(att[:], v_mx, tile_cols(n), wo_mx, cols, 2)
                 nc.vector.scalar_tensor_tensor(
-                    out=u[:, cols], in0=att[k], scalar=1.0, in1=liq_raw[q][:, i, cols],
+                    out=u[:, cols], in0=att[:], scalar=1.0, in1=residual[n][:, cols],
                     op0=ALU.mult, op1=ALU.add, accum_out=sums[:, k : k + 1],
                 )
             minus_mean = small.tile([P, 1], F32, tag="minus_mean")
@@ -259,11 +246,13 @@ def tile_advancedliquidneuralnetwork_pb_kernel(
 
         def add_xin_and_tanh(n):
             y = y_of[n]
-            xin = batch_major(xin_t, n)
+            xin = [psum.tile([P, 4, P], F32, name="xin%d" % k, tag="bank") for k in range(2)]
+            for j in range(8):
+                nc.tensor.transpose(xin[j // 4][:, j % 4, :], xin_t[:, j, tile_cols(n)], ident[:])
             for k, cols in enumerate(bank_cols):
                 nc.vector.scalar_tensor_tensor(
-                    out=y[:, cols], in0=y[:, cols], scalar=rstd_of[n][:], in1=xin[k],
-                    op0=ALU.mult, op1=ALU.add,
+                    out=y[:, cols], in0=y[:, cols], scalar=rstd_of[n][:],
+                    in1=xin[k][:].rearrange("p a r -> p (a r)"), op0=ALU.mult, op1=ALU.add,
                 )
             nc.scalar.activation(out=y[:], in_=y[:], func=ACT.Tanh)
 
@@ -276,23 +265,13 @@ def tile_advancedliquidneuralnetwork_pb_kernel(
             nc.vector.tensor_tensor(out=y[:], in0=y[:], in1=kept_of[n][:], op=ALU.add)
             nc.sync.dma_start(out=out_rows[q][:, i, :], in_=y[:])
 
-        def step(n):
-            if n < 8:
-                statistics(n)
-            if 0 <= n - 1 < 8:
-                centre_and_scale(n - 1)
-            if 0 <= n - 2 < 8:
-                times_r(n - 2)
-            if 0 <= n - 1 < 8:
-                add_xin_and_tanh(n - 1)
-            if 0 <= n - 2 < 8:
-                add_kept_and_store(n - 2)
-
         prepare_k1024(liq_raw[0], liq_mx, 0)
         spread_vectors()
+        prepare_k1024(liq_raw[1], liq_mx, 1)
+        for n in range(8):
+            add_bias_to_liq(n)
         for g in range(2):
             prepare_k1024(wv_raw[g], wv_mx, g)
-        prepare_k1024(liq_raw[1], liq_mx, 1)
 
         win_raw = raw.tile([P, 8, IN], BF16, tag="raw")
         x_raw = raw.tile([P, 8, IN], BF16, tag="raw")
@@ -301,20 +280,36 @@ def tile_advancedliquidneuralnetwork_pb_kernel(
             out=x_raw[:].rearrange("p (q i) k -> p q i k", q=2),
             in_=x.rearrange("(q p i) k -> p q i k", q=2, i=TILES),
         )
+        beta_t = consts.tile([P, 8], BF16)
+        bin_t = consts.tile([P, 8], BF16)
+        with nc.allow_non_contiguous_dma(reason="two vectors of 1024, one element a partition"):
+            nc.sync.dma_start(out=beta_t[:], in_=beta_att.rearrange("(j p) -> p j", p=P))
+            nc.sync.dma_start(out=bin_t[:], in_=b_in.rearrange("(j p) -> p j", p=P))
+
+        prepare_k1024(wo_raw[0], wo_mx, 0)
         compute_v(0)
-        for q in range(2):
-            prepare_k1024(wo_raw[q], wo_mx, q)
+        compute_v(1)
+        prepare_k1024(wo_raw[1], wo_mx, 1)
         h_raw = [raw.tile([P, TILES, H], BF16, name="h_raw%d" % q, tag="raw") for q in range(2)]
         for q in range(2):
             nc.sync.dma_start(out=h_raw[q][:], in_=h_rows[q])
-        feature_major(att_t, wo_mx, v_mx, 2, att_bias, 0)
-        compute_v(1)
-        step(0)
+        compute_v(2)
+        compute_v(3)
         prepare_k512(win_raw, win_mx)
         prepare_k512(x_raw, x_mx)
-        feature_major(xin_t, win_mx, x_mx, 1, xin_bias, 0)
-        step(1)
-        feature_major(att_t, wo_mx, v_mx, 2, att_bias, 1)
-        feature_major(xin_t, win_mx, x_mx, 1, xin_bias, 1)
-        for n in range(2, 10):
-            step(n)
+        nc.vector.tensor_tensor(out=xin_bias[:], in0=beta_t[:], in1=bin_t[:], op=ALU.add)
+
+        for n in range(8 + 2):
+            if n < 8:
+                statistics(n)
+            if n < TILES:
+                compute_xin(n // 2, range(4 * (n % 2), 4 * (n % 2) + 4))
+                compute_v(n + TILES)
+            if 0 <= n - 1 < 8:
+                centre_and_scale(n - 1)
+            if 0 <= n - 2 < 8:
+                times_r(n - 2)
+            if 0 <= n - 1 < 8:
+                add_xin_and_tanh(n - 1)
+            if 0 <= n - 2 < 8:
+                add_kept_and_store(n - 2)

from contextlib import ExitStack

import concourse.mybir as mybir
from concourse.masks import make_identity

F32 = mybir.dt.float32
BF16 = mybir.dt.bfloat16
U32 = mybir.dt.uint32
U8 = mybir.dt.uint8
FP8X4 = mybir.dt.float8_e4m3fn_x4
ALU = mybir.AluOpType
ACT = mybir.ActivationFunctionType

P = 128
B, IN, H = 1024, 512, 1024
K_PASS = 512
BANK = 512
CHUNK = 512
TILES = CHUNK // P
LN_EPS = 1e-5
TAU_EPS = 1e-6
SQRT_H = 32.0

FLOPS = 2 * B * H * (IN + H + H)


def tile_advancedliquidneuralnetwork_pb_kernel(
    tc, liq, h, x, W_in, b_in, W_v, b_v, W_o, b_o, g_att, beta_att, tau, out
):
    nc = tc.nc
    with ExitStack() as ctx:
        consts = ctx.enter_context(tc.tile_pool(name="consts", bufs=1))
        keep = ctx.enter_context(tc.tile_pool(name="keep", bufs=1))
        raw = ctx.enter_context(tc.tile_pool(name="raw", bufs=4))
        stage = ctx.enter_context(tc.tile_pool(name="stage", bufs=2))
        work = ctx.enter_context(tc.tile_pool(name="work", bufs=3))
        small = ctx.enter_context(tc.tile_pool(name="small", bufs=4))
        psum = ctx.enter_context(tc.psum_pool(name="psum", bufs=8))

        ident = consts.tile([P, P], F32)
        make_identity(nc, ident[:])
        ones = consts.tile([P, P], BF16)
        nc.vector.memset(ones[:], 1.0)
        minus_half = consts.tile([P, 1], F32)
        nc.vector.memset(minus_half[:], -0.5)

        bv = consts.tile([P, 8], BF16)
        nc.scalar.dma_start(
            out=bv[:].rearrange("p (c e) -> p c e", e=2),
            in_=b_v.rearrange("(c p e) -> p c e", p=P, e=2),
        )

        vec_rows = stage.tile([P, 3, H], BF16, tag="staged", align_bytes=64)
        nc.vector.memset(vec_rows[:], 0.0)
        for n, vector in enumerate((b_o, g_att, tau)):
            nc.scalar.dma_start(
                out=vec_rows[0:1, n, :], in_=vector.rearrange("(o n) -> o n", o=1)
            )

        warm = consts.tile([P, 2], F32)
        nc.vector.memset(warm[:], 0.0)
        nc.scalar.activation(out=warm[:, 1:2], in_=warm[:, 0:1], func=ACT.Tanh)

        liq_rows = liq.rearrange("(q p i) k -> q p i k", q=2, i=TILES)
        h_rows = h.rearrange("(q p i) k -> q p i k", q=2, i=TILES)
        out_rows = out.rearrange("(q p i) n -> q p i n", q=2, i=TILES)
        wv_rows = W_v.rearrange("(g u p e) k -> g p u e k", g=2, u=2, e=2)
        wo_rows = W_o.rearrange("(q j p) k -> q p j k", q=2, p=P)

        liq_raw = [keep.tile([P, TILES, H], BF16, name="liq_raw%d" % q) for q in range(2)]
        wv_raw = [raw.tile([P, TILES, H], BF16, name="wv_raw%d" % g, tag="raw") for g in range(2)]
        wo_raw = [raw.tile([P, TILES, H], BF16, name="wo_raw%d" % q, tag="raw") for q in range(2)]
        for q in range(2):
            nc.sync.dma_start(out=liq_raw[q][:], in_=liq_rows[q])
        for g in range(2):
            nc.sync.dma_start(
                out=wv_raw[g][:].rearrange("p (u e) k -> p u e k", e=2), in_=wv_rows[g]
            )
        for q in range(2):
            nc.sync.dma_start(out=wo_raw[q][:], in_=wo_rows[q])

        bo_all = consts.tile([P, H], BF16)
        g_all = consts.tile([P, H], BF16)
        r_all = consts.tile([P, H], F32)
        one_minus_r = consts.tile([P, H], F32)

        def spread_vectors():
            for half in range(2):
                cols = slice(half * BANK, (half + 1) * BANK)
                spread = [
                    psum.tile([P, BANK], F32, name="spread%d" % n, tag="bank") for n in range(3)
                ]
                for n in range(3):
                    nc.tensor.matmul(
                        spread[n][:], lhsT=ones[:], rhs=vec_rows[:, n, cols], start=True, stop=True
                    )
                nc.scalar.copy(out=bo_all[:, cols], in_=spread[0][:])
                nc.scalar.mul(out=g_all[:, cols], in_=spread[1][:], mul=SQRT_H)
                nc.vector.tensor_scalar_add(out=r_all[:, cols], in0=spread[2][:], scalar1=TAU_EPS)
            nc.vector.reciprocal(out=r_all[:], in_=r_all[:])
            nc.gpsimd.tensor_scalar(
                out=one_minus_r[:], in0=r_all[:], scalar1=-1.0, scalar2=1.0,
                op0=ALU.mult, op1=ALU.add,
            )

        def mx_operand(name, passes):
            codes = keep.tile([P, passes, 1024], U32, name=name + "_codes", align_bytes=64)
            scales = keep.tile([P, passes, 1024], U8, name=name + "_scales", align_bytes=64)
            return codes, scales

        liq_mx = mx_operand("liq", 2)
        wv_mx = mx_operand("wv", 2)
        v_mx = mx_operand("v", 2)
        wo_mx = mx_operand("wo", 2)
        x_mx = mx_operand("x", 1)
        win_mx = mx_operand("win", 1)

        def transpose_four(word_blocks, grouped_words):
            bank = psum.tile([P, 4, P], F32, tag="bank")
            for n, block in enumerate(word_blocks):
                nc.tensor.transpose(bank[:, n, :], block, ident[:])
            nc.scalar.copy(out=grouped_words, in_=bank[:].rearrange("p (a u) r -> p a r u", u=2))

        def quantise(grouped, c, operand, cols):
            codes, scales = operand
            nc.vector.quantize_mx(
                out=codes[:, c, cols].bitcast(FP8X4),
                scales=scales[:, c, cols],
                in_=grouped[:, c, :, :].rearrange("p r t -> p (r t)"),
            )

        def prepare_k1024(rows_raw, operand, chunk):
            words = rows_raw[:].bitcast(F32)
            grouped = stage.tile([P, 2, CHUNK, 4], BF16, tag="staged", align_bytes=64)
            grouped_words = grouped[:].bitcast(F32)
            for i in range(TILES):
                transpose_four(
                    [words[:, i, w * P : (w + 1) * P] for w in range(4)],
                    grouped_words[:, :, i * P : (i + 1) * P, :],
                )
            for c in range(2):
                quantise(grouped, c, operand, slice(chunk * CHUNK, (chunk + 1) * CHUNK))

        def prepare_k512(rows_raw, operand):
            words = rows_raw[:].bitcast(F32)
            grouped = stage.tile([P, 1, 1024, 4], BF16, tag="staged", align_bytes=64)
            grouped_words = grouped[:].bitcast(F32)
            for j in range(0, 8, 2):
                transpose_four(
                    [words[:, j + a, u * P : (u + 1) * P] for a in range(2) for u in range(2)],
                    grouped_words[:, 0, j * P : (j + 2) * P, :].rearrange(
                        "p (a r) u -> p a r u", a=2
                    ),
                )
            quantise(grouped, 0, operand, slice(0, 1024))

        def mx_matmul(acc, stationary, s_cols, moving, m_cols, passes):
            for c in range(passes):
                nc.tensor.matmul_mx(
                    out=acc,
                    lhsT=stationary[0][:, c, s_cols].bitcast(FP8X4),
                    lhsT_scale=stationary[1][:, c, s_cols],
                    rhs=moving[0][:, c, m_cols].bitcast(FP8X4),
                    rhs_scale=moving[1][:, c, m_cols],
                    start=(c == 0),
                    stop=(c == passes - 1),
                )

        def tile_cols(n):
            return slice(n * P, (n + 1) * P)

        def compute_v(n):
            grouped = stage.tile([P, 2, P, 4], BF16, tag="v_grouped", bufs=3, align_bytes=64)
            for g in range(2):
                bank = psum.tile([P, 4, P], F32, tag="bank")
                for t in range(4):
                    mx_matmul(bank[:, t, :], wv_mx, tile_cols(4 * g + t), liq_mx, tile_cols(n), 2)
                nc.vector.tensor_tensor(
                    out=grouped[:, g, :, :],
                    in0=bank[:].rearrange("p t r -> p r t"),
                    in1=bv[:, 4 * g : 4 * g + 4].unsqueeze(1).to_broadcast([P, P, 4]),
                    op=ALU.add,
                )
            for g in range(2):
                quantise(grouped, g, v_mx, tile_cols(n))

        xin_t = keep.tile([P, 8, B], F32)
        xin_bias = consts.tile([P, 8], F32)

        def compute_xin(q, features):
            cols = slice(q * CHUNK, (q + 1) * CHUNK)
            for j in features:
                bank = psum.tile([P, BANK], F32, tag="bank")
                mx_matmul(bank[:], win_mx, tile_cols(j), x_mx, cols, 1)
                nc.scalar.activation(
                    out=xin_t[:, j, cols], in_=bank[:], func=ACT.Identity,
                    bias=xin_bias[:, j : j + 1], scale=1.0,
                )

        residual, u_of, y_of, minus_mean_of, rstd_of, kept_of = {}, {}, {}, {}, {}, {}
        bank_cols = [slice(k * BANK, (k + 1) * BANK) for k in range(2)]

        def add_bias_to_liq(n):
            q, i = divmod(n, TILES)
            residual[n] = work.tile([P, H], F32, name="residual", tag="residual", bufs=8)
            nc.gpsimd.tensor_tensor(
                out=residual[n][:], in0=liq_raw[q][:, i, :], in1=bo_all[:], op=ALU.add
            )

        def statistics(n):
            u = work.tile([P, H], F32, tag="u", bufs=2)
            y = work.tile([P, H], F32, tag="y", bufs=4)
            sums = small.tile([P, 2], F32, tag="sums")
            for k, cols in enumerate(bank_cols):
                att = psum.tile([P, BANK], F32, tag="bank")
                mx_matmul(att[:], v_mx, tile_cols(n), wo_mx, cols, 2)
                nc.vector.scalar_tensor_tensor(
                    out=u[:, cols], in0=att[:], scalar=1.0, in1=residual[n][:, cols],
                    op0=ALU.mult, op1=ALU.add, accum_out=sums[:, k : k + 1],
                )
            minus_mean = small.tile([P, 1], F32, tag="minus_mean")
            nc.vector.tensor_scalar(
                out=minus_mean[:], in0=sums[:, 0:1], scalar1=sums[:, 1:2], scalar2=-1.0 / H,
                op0=ALU.add, op1=ALU.mult,
            )
            square_sum = small.tile([P, 1], F32, tag="square_sum")
            nc.scalar.activation(
                out=y[:], in_=u[:], func=ACT.Square, bias=minus_mean[:], scale=1.0,
                accum_out=square_sum[:],
            )
            rstd = small.tile([P, 1], F32, tag="rstd")
            nc.gpsimd.tensor_scalar_add(out=rstd[:], in0=square_sum[:], scalar1=H * LN_EPS)
            nc.gpsimd.tensor_tensor(out=rstd[:], in0=rstd[:], in1=minus_half[:], op=ALU.pow)
            u_of[n], y_of[n], minus_mean_of[n], rstd_of[n] = u, y, minus_mean, rstd

        def centre_and_scale(n):
            q, i = divmod(n, TILES)
            kept_of[n] = work.tile([P, H], F32, name="kept", tag="kept", bufs=2)
            nc.gpsimd.tensor_tensor(
                out=kept_of[n][:], in0=h_raw[q][:, i, :], in1=one_minus_r[:], op=ALU.mult
            )
            nc.vector.scalar_tensor_tensor(
                out=y_of[n][:], in0=u_of[n][:], scalar=minus_mean_of[n][:], in1=g_all[:],
                op0=ALU.add, op1=ALU.mult,
            )

        def add_xin_and_tanh(n):
            y = y_of[n]
            xin = [psum.tile([P, 4, P], F32, name="xin%d" % k, tag="bank") for k in range(2)]
            for j in range(8):
                nc.tensor.transpose(xin[j // 4][:, j % 4, :], xin_t[:, j, tile_cols(n)], ident[:])
            for k, cols in enumerate(bank_cols):
                nc.vector.scalar_tensor_tensor(
                    out=y[:, cols], in0=y[:, cols], scalar=rstd_of[n][:],
                    in1=xin[k][:].rearrange("p a r -> p (a r)"), op0=ALU.mult, op1=ALU.add,
                )
            nc.scalar.activation(out=y[:], in_=y[:], func=ACT.Tanh)

        def times_r(n):
            nc.vector.tensor_tensor(out=y_of[n][:], in0=y_of[n][:], in1=r_all[:], op=ALU.mult)

        def add_kept_and_store(n):
            q, i = divmod(n, TILES)
            y = y_of[n]
            nc.vector.tensor_tensor(out=y[:], in0=y[:], in1=kept_of[n][:], op=ALU.add)
            nc.sync.dma_start(out=out_rows[q][:, i, :], in_=y[:])

        prepare_k1024(liq_raw[0], liq_mx, 0)
        spread_vectors()
        prepare_k1024(liq_raw[1], liq_mx, 1)
        for n in range(8):
            add_bias_to_liq(n)
        for g in range(2):
            prepare_k1024(wv_raw[g], wv_mx, g)

        win_raw = raw.tile([P, 8, IN], BF16, tag="raw")
        x_raw = raw.tile([P, 8, IN], BF16, tag="raw")
        nc.sync.dma_start(out=win_raw[:], in_=W_in.rearrange("(j p) k -> p j k", p=P))
        nc.sync.dma_start(
            out=x_raw[:].rearrange("p (q i) k -> p q i k", q=2),
            in_=x.rearrange("(q p i) k -> p q i k", q=2, i=TILES),
        )
        beta_t = consts.tile([P, 8], BF16)
        bin_t = consts.tile([P, 8], BF16)
        with nc.allow_non_contiguous_dma(reason="two vectors of 1024, one element a partition"):
            nc.sync.dma_start(out=beta_t[:], in_=beta_att.rearrange("(j p) -> p j", p=P))
            nc.sync.dma_start(out=bin_t[:], in_=b_in.rearrange("(j p) -> p j", p=P))

        prepare_k1024(wo_raw[0], wo_mx, 0)
        compute_v(0)
        compute_v(1)
        prepare_k1024(wo_raw[1], wo_mx, 1)
        h_raw = [raw.tile([P, TILES, H], BF16, name="h_raw%d" % q, tag="raw") for q in range(2)]
        for q in range(2):
            nc.sync.dma_start(out=h_raw[q][:], in_=h_rows[q])
        compute_v(2)
        compute_v(3)
        prepare_k512(win_raw, win_mx)
        prepare_k512(x_raw, x_mx)
        nc.vector.tensor_tensor(out=xin_bias[:], in0=beta_t[:], in1=bin_t[:], op=ALU.add)

        for n in range(8 + 2):
            if n < 8:
                statistics(n)
            if n < TILES:
                compute_xin(n // 2, range(4 * (n % 2), 4 * (n % 2) + 4))
                compute_v(n + TILES)
            if 0 <= n - 1 < 8:
                centre_and_scale(n - 1)
            if 0 <= n - 2 < 8:
                times_r(n - 2)
            if 0 <= n - 1 < 8:
                add_xin_and_tanh(n - 1)
            if 0 <= n - 2 < 8:
                add_kept_and_store(n - 2)
